import numpy as np
import ml_dtypes


def mxq(x, axis, fmt="e4m3"):
    dtype, down = {"e4m3": (ml_dtypes.float8_e4m3fn, 7), "e5m2": (ml_dtypes.float8_e5m2, 14)}[fmt]
    v = np.moveaxis(np.asarray(x, np.float32).astype(ml_dtypes.bfloat16).astype(np.float64), axis, -1)
    blocks = v.reshape(v.shape[:-1] + (-1, 32))
    amax = np.abs(blocks).max(-1, keepdims=True)
    byte = np.maximum(np.where(amax > 0, np.frexp(amax)[1] - 1 + 127, 0) - down, 1)
    scale = np.exp2(byte - 127.0)
    codes = (blocks / scale).astype(np.float32).astype(dtype).astype(np.float64)
    return np.moveaxis((codes * scale).reshape(v.shape), -1, axis)


WIDE = False


def mx_kscale(k):
    if not WIDE:
        return np.ones(k)
    levels = np.array([10, -10, 5, -5, 0])
    if k % 512:
        return np.exp2(np.random.permutation(np.resize(levels, k // 32))).repeat(32)
    a = np.empty((k // 512, 16))
    for p in range(k // 512):
        a[p, :8] = np.random.permutation(np.resize(levels, 8))
        for g in range(8):
            far = levels[np.abs(levels - a[p, g]) >= 10]
            a[p, g + 8] = far[np.random.randint(len(far))]
    return np.exp2(a.ravel()).repeat(32)


BF16 = ml_dtypes.bfloat16


def bf(x):
    return np.asarray(x, np.float32).astype(BF16)


def f64(x):
    return np.asarray(x).astype(np.float64)


B, S, HIDDEN, NH, NKV, HD, WINDOW = 1, 1024, 1024, 8, 4, 256, 512
Q_SIZE, KV_SIZE = NH * HD, NKV * HD
O_SIZE = Q_SIZE + KV_SIZE + KV_SIZE
EPS = 1e-6
ROPE_THETA = 10000.0


def rms_norm(u, w):
    var = np.mean(np.square(u), axis=-1, keepdims=True)
    return u / np.sqrt(var + EPS) * (1.0 + w)


def rope(u, cos, sin):
    d2 = u.shape[-1] // 2
    u1, u2 = u[..., :d2], u[..., d2:]
    c = cos[None, :, None, :]
    s = sin[None, :, None, :]
    return np.concatenate([u1 * c - u2 * s, u1 * s + u2 * c], axis=-1)


def draw0():
    s = mx_kscale(HIDDEN)
    inv_freq = 1.0 / ROPE_THETA ** (np.arange(0, HD, 2) / HD)
    ang = np.arange(S)[:, None] * inv_freq[None, :]
    return {"x": bf(np.random.standard_normal((B, S, HIDDEN)) * s),
            "qkv_w": bf(np.random.standard_normal((O_SIZE, HIDDEN)) / np.sqrt(HIDDEN) / s[None, :]),
            "q_norm_w": bf(1.0 + 0.3 * np.random.standard_normal(HD)),
            "k_norm_w": bf(1.0 + 0.3 * np.random.standard_normal(HD)),
            "freqs_cos": bf(np.cos(ang)),
            "freqs_sin": bf(np.sin(ang))}


def core(x, qkv_w, q_norm_w, k_norm_w, freqs_cos, freqs_sin):
    qkv = mxq(f64(x), 2, "e4m3") @ mxq(f64(qkv_w), 1, "e4m3").T
    q = qkv[..., :Q_SIZE].reshape(B, S, NH, HD)
    k = qkv[..., Q_SIZE:Q_SIZE + KV_SIZE].reshape(B, S, NKV, HD)
    v = qkv[..., Q_SIZE + KV_SIZE:].reshape(B, S, NKV, HD)
    q = rms_norm(q, f64(q_norm_w))
    k = rms_norm(k, f64(k_norm_w))
    q = rope(q, f64(freqs_cos), f64(freqs_sin))
    k = rope(k, f64(freqs_cos), f64(freqs_sin))
    return q, k, v


def e4m3fn_bytes(y):
    return np.clip(np.asarray(y, np.float64), -448.0, 448.0).astype(np.float32).astype(ml_dtypes.float8_e4m3fn).view(np.uint8)


def e4m3fn_values(b):
    return np.asarray(b, np.uint8).view(ml_dtypes.float8_e4m3fn).astype(np.float64)


def setup_inputs():
    d = draw0()
    x0 = np.asarray(d['qkv_w']).astype(np.float64)
    s = (np.max(np.abs(x0), axis=(0,), keepdims=True) / 448.0).astype(np.float32)
    out = {}
    for k, v in d.items():
        if k == 'qkv_w':
            out['qkv_w_bytes'] = e4m3fn_bytes(x0 / s.astype(np.float64))
            out['qkv_w_scale'] = s
        else:
            out[k] = v
    return out


def reference(x, qkv_w_bytes, qkv_w_scale, q_norm_w, k_norm_w, freqs_cos, freqs_sin):
    return core(x, e4m3fn_values(qkv_w_bytes) * qkv_w_scale.astype(np.float64), q_norm_w, k_norm_w, freqs_cos, freqs_sin)

@@ -1,0 +1,314 @@
+from contextlib import ExitStack
+
+import concourse.mybir as mybir
+from concourse.masks import make_identity
+
+F32 = mybir.dt.float32
+BF16 = mybir.dt.bfloat16
+U32 = mybir.dt.uint32
+U8 = mybir.dt.uint8
+FP8 = mybir.dt.float8_e4m3fn
+FP8X4 = mybir.dt.float8_e4m3fn_x4
+ALU = mybir.AluOpType
+ACT = mybir.ActivationFunctionType
+
+P = 128
+S = 1024
+K = 1024
+N = 4096
+HD = 256
+HALF = 128
+EPS = 1e-6
+PASSES = 2
+TOK_TILES = 8
+N_TILE = 512
+FLOPS = 2 * S * K * N
+
+HEAD_TILES = (0, 6)
+LOOP_TILES = (1, 2, 3, 7, 4, 5)
+PERIOD = 8
+LATE_ADDS = 3
+
+
+def tile_gemmaattention_pa_kernel(
+    tc, x, qkv_w_bytes, qkv_w_scale, q_norm_w, k_norm_w, freqs_cos, freqs_sin, out_0, out_1, out_2
+):
+    nc = tc.nc
+    x2 = x.rearrange("o s k -> (o s) k")
+    outs = (
+        out_0.rearrange("o s h d -> (o s) (h d)"),
+        out_1.rearrange("o s h d -> (o s) (h d)"),
+        out_2.rearrange("o s h d -> (o s) (h d)"),
+    )
+
+    with ExitStack() as ctx:
+        const = ctx.enter_context(tc.tile_pool(name="const", bufs=1))
+        wbfp = ctx.enter_context(tc.tile_pool(name="wbfp", bufs=8))
+        grp = ctx.enter_context(tc.tile_pool(name="grp", bufs=4))
+        epi = ctx.enter_context(tc.tile_pool(name="epi", bufs=4))
+        stat = ctx.enter_context(tc.tile_pool(name="stat", bufs=6))
+        tpp = ctx.enter_context(tc.psum_pool(name="tpp", bufs=3))
+        accp = ctx.enter_context(tc.psum_pool(name="accp", bufs=5))
+        ctx.enter_context(tc.manual_schedule())
+
+        s4 = const.tile([P, PASSES, 4], F32, name="s4")
+        nc.scalar.dma_start(out=s4[:], in_=qkv_w_scale.rearrange("o (g p t) -> p (o g) t", p=P, t=4))
+        cosb = const.tile([P, TOK_TILES, HALF], BF16, name="cosb")
+        sinb = const.tile([P, TOK_TILES, HALF], BF16, name="sinb")
+        nc.scalar.dma_start(out=cosb[:], in_=freqs_cos.rearrange("(i p) d -> p i d", p=P))
+        nc.scalar.dma_start(out=sinb[:], in_=freqs_sin.rearrange("(i p) d -> p i d", p=P))
+        raw = {}
+        for tag, nw in (("q", q_norm_w), ("k", k_norm_w)):
+            raw[tag] = const.tile([P, HD], BF16, name="graw" + tag)
+            nc.scalar.dma_start(out=raw[tag][:], in_=nw.partition_broadcast(P))
+
+        wb = {}
+        xr = {}
+
+        def load_w(j, pieces):
+            wb[j] = const.tile([P, 4, K], U8, name="wb%d" % j)
+            rt = 4 // pieces
+            for c in range(pieces):
+                nc.sync.dma_start(
+                    out=wb[j][:, c * rt : (c + 1) * rt, :],
+                    in_=qkv_w_bytes[j * N_TILE + c * rt * P : j * N_TILE + (c + 1) * rt * P, :].rearrange(
+                        "(r p) k -> p r k", p=P
+                    ),
+                )
+
+        load_w(HEAD_TILES[0], 2)
+        load_w(HEAD_TILES[1], 1)
+        for i in range(TOK_TILES):
+            xr[i] = const.tile([P, K], BF16, name="xr%d" % i)
+            nc.sync.dma_start(out=xr[i][:], in_=x2[i * P : (i + 1) * P, :])
+        for j in LOOP_TILES:
+            load_w(j, 1)
+
+        one = const.tile([P, 1], F32, name="one")
+        nc.vector.memset(one[:], 1.0)
+        warm = const.tile([P, 1], F32, name="warm")
+        nc.scalar.activation(out=warm[:], in_=one[:], func=ACT.Abs_reciprocal_sqrt)
+        ident = const.tile([P, P], F32, name="ident")
+        make_identity(nc, ident[:])
+
+        tabs = {}
+        gains = {}
+        for tag in ("q", "k"):
+            tabs[tag] = const.tile([P, TOK_TILES, 2 * HD], F32, name="tab" + tag)
+
+        def make_gains(tag):
+            gp = const.tile([P, HD], F32, name="gp" + tag)
+            nc.gpsimd.tensor_scalar(out=gp[:], in0=raw[tag][:], scalar1=1.0, scalar2=1.0, op0=ALU.mult, op1=ALU.add)
+            gm = const.tile([P, HD], F32, name="gm" + tag)
+            nc.gpsimd.tensor_scalar(
+                out=gm[:, 0:HALF], in0=raw[tag][:, 0:HALF], scalar1=1.0, scalar2=1.0, op0=ALU.mult, op1=ALU.add
+            )
+            nc.gpsimd.tensor_scalar(
+                out=gm[:, HALF:HD], in0=raw[tag][:, HALF:HD], scalar1=-1.0, scalar2=-1.0, op0=ALU.mult, op1=ALU.add
+            )
+            gains[tag] = (gp, gm)
+
+        def table_chunk(tag, i0, part):
+            trig = (cosb, sinb)[part]
+            nc.gpsimd.tensor_tensor(
+                out=tabs[tag][:, i0 : i0 + 2, part * HD : (part + 1) * HD].rearrange("p i (a d) -> p i a d", a=2),
+                in0=trig[:, i0 : i0 + 2, :].unsqueeze(2).to_broadcast([P, 2, 2, HALF]),
+                in1=gains[tag][part][:].rearrange("p (a d) -> p a d", a=2).unsqueeze(1).to_broadcast([P, 2, 2, HALF]),
+                op=ALU.mult,
+            )
+
+        chunks = [(tag, i0, part) for tag in ("q", "k") for i0 in range(0, TOK_TILES, 2) for part in range(2)]
+        make_gains("q")
+        for n in range(4):
+            table_chunk(*chunks[n])
+        chunks = chunks[4:]
+
+        xq = {}
+        xs = {}
+        for half in range(2):
+            xq[half] = const.tile([P, 2, PASSES, 2 * P], U32, name="xq%d" % half, align_bytes=64)
+            xs[half] = const.tile([P, 2, PASSES, 2 * P], U8, name="xs%d" % half, align_bytes=64)
+        wq = {}
+        ws = {}
+        for j in range(8):
+            wq[j] = const.tile([P, PASSES, N_TILE], U32, name="wq%d" % j, align_bytes=64)
+            ws[j] = const.tile([P, PASSES, N_TILE], U8, name="ws%d" % j, align_bytes=64)
+
+        def turn(tiles, g):
+            tp = tpp.tile([P, 2, 2 * P], F32, name="tp", tag="tp")
+            for a in range(2):
+                words = tiles[a][:].bitcast(F32)
+                for u in range(2):
+                    nc.tensor.transpose(
+                        tp[:, u, a * P : (a + 1) * P], words[:, 256 * g + u : 256 * (g + 1) : 2], ident[:]
+                    )
+            return tp
+
+        def x_half(half):
+            xg = grp.tile([P, 8 * N_TILE], BF16, name="grouped", tag="grouped", align_bytes=64)
+            for pr in range(2):
+                for g in range(PASSES):
+                    tp = turn((xr[half * 4 + pr * 2], xr[half * 4 + pr * 2 + 1]), g)
+                    c0 = (pr * PASSES + g) * 512
+                    nc.scalar.copy(
+                        out=xg[:].bitcast(F32)[:, c0 : c0 + 512].rearrange("p (r u) -> p r u", u=2),
+                        in_=tp[:].rearrange("p u r -> p r u"),
+                    )
+            nc.vector.quantize_mx(
+                out=xq[half][:].rearrange("p a g c -> p (a g c)").bitcast(FP8X4),
+                scales=xs[half][:].rearrange("p a g c -> p (a g c)"),
+                in_=xg[:],
+            )
+
+        wbf = {}
+        wgr = {}
+
+        def w_cast(j, r, engine):
+            wbf[(j, r)] = wbfp.tile([P, K], BF16, name="wbf", tag="wbf")
+            src = wb[j][:, r, :].bitcast(FP8)
+            if engine == "vector":
+                nc.vector.tensor_copy(out=wbf[(j, r)][:], in_=src)
+            else:
+                nc.scalar.copy(out=wbf[(j, r)][:], in_=src)
+
+        def w_turn(j, g, pr):
+            if (g, pr) == (0, 0):
+                wgr[j] = grp.tile([P, 8 * N_TILE], BF16, name="grouped", tag="grouped", align_bytes=64)
+            tp = turn((wbf[(j, pr * 2)], wbf[(j, pr * 2 + 1)]), g)
+            c0 = g * 2048 + pr * 1024
+            nc.vector.tensor_tensor(
+                out=wgr[j][:, c0 : c0 + 1024].rearrange("p (n u e) -> p n u e", u=2, e=2),
+                in0=tp[:].bitcast(BF16).rearrange("p u (n e) -> p n u e", e=2),
+                in1=s4[:, g, :].rearrange("p (o u e) -> p o u e", o=1, u=2).to_broadcast([P, 2 * P, 2, 2]),
+                op=ALU.mult,
+            )
+
+        def w_quant(j):
+            nc.vector.quantize_mx(
+                out=wq[j][:].rearrange("p g c -> p (g c)").bitcast(FP8X4),
+                scales=ws[j][:].rearrange("p g c -> p (g c)"),
+                in_=wgr[j][:],
+            )
+
+        def step(i, j, quant_tile, late_add):
+            acc = accp.tile([P, N_TILE], F32, name="acc", tag="acc")
+            rows = slice(i * P, (i + 1) * P)
+            cols = slice((i % 2) * P, (i % 2 + 1) * P)
+            for g in range(PASSES):
+                nc.tensor.matmul_mx(
+                    out=acc[:],
+                    lhsT=xq[i // 4][:, (i % 4) // 2, g, cols].bitcast(FP8X4),
+                    lhsT_scale=xs[i // 4][:, (i % 4) // 2, g, cols],
+                    rhs=wq[j][:, g, :].bitcast(FP8X4),
+                    rhs_scale=ws[j][:, g, :],
+                    start=(g == 0),
+                    stop=(g == PASSES - 1),
+                )
+            if j >= 6:
+                res = epi.tile([P, N_TILE], F32, name="resv", tag="resv", bufs=3)
+                nc.scalar.copy(out=res[:], in_=acc[:])
+                dst = outs[2][rows, (j - 6) * N_TILE : (j - 5) * N_TILE]
+            else:
+                tab = tabs["q" if j < 4 else "k"]
+                ms = stat.tile([P, 2], F32, name="ms", tag="ms")
+                for h in range(2):
+                    junk = stat.tile([P, HD], BF16, name="junk", tag="junk")
+                    nc.scalar.activation(
+                        out=junk[:],
+                        in_=acc[:, h * HD : (h + 1) * HD],
+                        func=ACT.Square,
+                        scale=0.0625,
+                        accum_out=ms[:, h : h + 1],
+                    )
+                rs = stat.tile([P, 2], F32, name="rs", tag="rs")
+                nc.scalar.activation(out=rs[:], in_=ms[:], func=ACT.Abs_reciprocal_sqrt, bias=EPS, scale=1.0)
+                pq = epi.tile([P, 2, 2, 2, HALF], F32, name="pq", tag="pq")
+                for h in range(2):
+                    nc.vector.scalar_tensor_tensor(
+                        out=pq[:, h].rearrange("p r a d -> p r (a d)"),
+                        in0=acc[:, h * HD : (h + 1) * HD].unsqueeze(1).to_broadcast([P, 2, HD]),
+                        scalar=rs[:, h : h + 1],
+                        in1=tab[:, i, :].rearrange("p (r c) -> p r c", r=2),
+                        op0=ALU.mult,
+                        op1=ALU.mult,
+                    )
+                    if h == 0 and quant_tile is not None:
+                        w_quant(quant_tile)
+                if j < 4:
+                    dst = outs[0][rows, j * N_TILE : (j + 1) * N_TILE]
+                else:
+                    dst = outs[1][rows, (j - 4) * N_TILE : (j - 3) * N_TILE]
+                if late_add:
+                    late.append((pq, dst))
+                    return
+                res = epi.tile([P, N_TILE], F32, name="res", tag="res")
+                add_halves(nc.gpsimd, res, pq)
+            nc.sync.dma_start(out=dst, in_=res[:])
+
+        def add_halves(engine, res, pq):
+            engine.tensor_tensor(
+                out=res[:].rearrange("p (h a d) -> p h a d", h=2, a=2),
+                in0=pq[:, :, 0, :, :],
+                in1=pq[:, :, 1, ::-1, :],
+                op=ALU.add,
+            )
+
+        late = []
+
+        j0, j1 = HEAD_TILES
+        w_cast(j0, 0, "vector")
+        w_cast(j0, 1, "vector")
+        w_cast(j0, 2, "scalar")
+        w_cast(j0, 3, "scalar")
+        for r in range(4):
+            w_cast(j1, r, "scalar")
+        for j in HEAD_TILES:
+            for pr in range(2):
+                for g in range(PASSES):
+                    w_turn(j, g, pr)
+        w_quant(j0)
+        x_half(0)
+        w_quant(j1)
+        x_half(1)
+        make_gains("k")
+
+        values = [(i, j) for j in (6, 7) for i in range(TOK_TILES)]
+        slots = []
+        for n in range(48):
+            slots.append((n % TOK_TILES, n // TOK_TILES))
+            if n % 3 == 2:
+                slots.append(values[n // 3])
+        rope_steps = 0
+        waiting = None
+        for n, slot in enumerate(slots):
+            i, j = slot
+            if j < 6:
+                step(i, j, waiting, rope_steps >= 48 - LATE_ADDS)
+                rope_steps += 1
+                if chunks and (rope_steps <= 2 or waiting is not None):
+                    table_chunk(*chunks[0])
+                    table_chunk(*chunks[1])
+                    chunks = chunks[2:]
+                waiting = None
+            else:
+                step(i, j, None, False)
+            if n // PERIOD < len(LOOP_TILES):
+                jn = LOOP_TILES[n // PERIOD]
+                phase = n % PERIOD
+                if phase == 0:
+                    w_cast(jn, 0, "scalar")
+                    w_cast(jn, 1, "scalar")
+                elif phase == 1:
+                    w_turn(jn, 0, 0)
+                    w_turn(jn, 1, 0)
+                    w_cast(jn, 2, "scalar")
+                    w_cast(jn, 3, "scalar")
+                elif phase == 6:
+                    w_turn(jn, 0, 1)
+                    w_turn(jn, 1, 1)
+                    waiting = jn
+        assert not chunks
+        for pq, dst in late:
+            res = epi.tile([P, N_TILE], F32, name="resw", tag="resw", bufs=LATE_ADDS)
+            add_halves(nc.vector, res, pq)
+            nc.sync.dma_start(out=dst, in_=res[:])

@@ -55,12 +55,18 @@ def tile_gemmaattention_pa_kernel(
         nc.scalar.dma_start(out=s4[:], in_=qkv_w_scale.rearrange("o (g p t) -> p (o g) t", p=P, t=4))
         cosb = const.tile([P, TOK_TILES, HALF], BF16, name="cosb")
         sinb = const.tile([P, TOK_TILES, HALF], BF16, name="sinb")
-        nc.scalar.dma_start(out=cosb[:], in_=freqs_cos.rearrange("(i p) d -> p i d", p=P))
-        nc.scalar.dma_start(out=sinb[:], in_=freqs_sin.rearrange("(i p) d -> p i d", p=P))
-        raw = {}
-        for tag, nw in (("q", q_norm_w), ("k", k_norm_w)):
-            raw[tag] = const.tile([P, HD], BF16, name="graw" + tag)
-            nc.scalar.dma_start(out=raw[tag][:], in_=nw.partition_broadcast(P))
+        wrow = const.tile([P, 2 * HD], BF16, name="wrow")
+        nc.gpsimd.memset(wrow[:], 0.0)
+        nc.scalar.dma_start(out=wrow[0:1, 0:HD], in_=q_norm_w.rearrange("(o d) -> o d", o=1))
+        nc.scalar.dma_start(out=wrow[0:1, HD : 2 * HD], in_=k_norm_w.rearrange("(o d) -> o d", o=1))
+        ones = const.tile([P, P], BF16, name="ones")
+        nc.gpsimd.memset(ones[:], 1.0)
+
+        def load_trig(i0):
+            for trig, src in ((cosb, freqs_cos), (sinb, freqs_sin)):
+                nc.sync.dma_start(
+                    out=trig[:, i0 : i0 + 4, :], in_=src.rearrange("(i p) d -> p i d", p=P)[:, i0 : i0 + 4, :]
+                )
 
         wb = {}
         xr = {}
@@ -77,10 +83,12 @@ def tile_gemmaattention_pa_kernel(
                 )
 
         load_w(HEAD_TILES[0], 2)
+        load_trig(0)
         load_w(HEAD_TILES[1], 1)
         for i in range(TOK_TILES):
             xr[i] = const.tile([P, K], BF16, name="xr%d" % i)
             nc.sync.dma_start(out=xr[i][:], in_=x2[i * P : (i + 1) * P, :])
+        load_trig(4)
         for j in LOOP_TILES:
             load_w(j, 1)
 
@@ -96,32 +104,36 @@ def tile_gemmaattention_pa_kernel(
         for tag in ("q", "k"):
             tabs[tag] = const.tile([P, TOK_TILES, 2 * HD], F32, name="tab" + tag)
 
+        gall = const.tile([P, 2, HD], F32, name="gall")
+
+        def spread_gains():
+            wall = accp.tile([P, 2 * HD], F32, name="acc", tag="acc")
+            nc.tensor.matmul(out=wall[:], lhsT=ones[:], rhs=wrow[:], start=True, stop=True)
+            nc.scalar.activation(
+                out=gall[:].rearrange("p t d -> p (t d)"), in_=wall[:], func=ACT.Copy, bias=1.0, scale=1.0
+            )
+
         def make_gains(tag):
-            gp = const.tile([P, HD], F32, name="gp" + tag)
-            nc.gpsimd.tensor_scalar(out=gp[:], in0=raw[tag][:], scalar1=1.0, scalar2=1.0, op0=ALU.mult, op1=ALU.add)
+            gp = gall[:, 0 if tag == "q" else 1, :]
             gm = const.tile([P, HD], F32, name="gm" + tag)
             nc.gpsimd.tensor_scalar(
-                out=gm[:, 0:HALF], in0=raw[tag][:, 0:HALF], scalar1=1.0, scalar2=1.0, op0=ALU.mult, op1=ALU.add
+                out=gm[:, 0:HALF], in0=gp[:, 0:HALF], scalar1=1.0, scalar2=0.0, op0=ALU.mult, op1=ALU.add
             )
             nc.gpsimd.tensor_scalar(
-                out=gm[:, HALF:HD], in0=raw[tag][:, HALF:HD], scalar1=-1.0, scalar2=-1.0, op0=ALU.mult, op1=ALU.add
+                out=gm[:, HALF:HD], in0=gp[:, HALF:HD], scalar1=-1.0, scalar2=0.0, op0=ALU.mult, op1=ALU.add
             )
-            gains[tag] = (gp, gm)
+            gains[tag] = (gp, gm[:])
 
         def table_chunk(tag, i0, part):
             trig = (cosb, sinb)[part]
             nc.gpsimd.tensor_tensor(
                 out=tabs[tag][:, i0 : i0 + 2, part * HD : (part + 1) * HD].rearrange("p i (a d) -> p i a d", a=2),
                 in0=trig[:, i0 : i0 + 2, :].unsqueeze(2).to_broadcast([P, 2, 2, HALF]),
-                in1=gains[tag][part][:].rearrange("p (a d) -> p a d", a=2).unsqueeze(1).to_broadcast([P, 2, 2, HALF]),
+                in1=gains[tag][part].rearrange("p (a d) -> p a d", a=2).unsqueeze(1).to_broadcast([P, 2, 2, HALF]),
                 op=ALU.mult,
             )
 
         chunks = [(tag, i0, part) for tag in ("q", "k") for i0 in range(0, TOK_TILES, 2) for part in range(2)]
-        make_gains("q")
-        for n in range(4):
-            table_chunk(*chunks[n])
-        chunks = chunks[4:]
 
         xq = {}
         xs = {}
@@ -260,12 +272,20 @@ def tile_gemmaattention_pa_kernel(
         w_cast(j0, 1, "vector")
         w_cast(j0, 2, "scalar")
         w_cast(j0, 3, "scalar")
+        for g in range(PASSES):
+            w_turn(j0, g, 0)
+        spread_gains()
+        make_gains("q")
+        for n in range(4):
+            table_chunk(*chunks[n])
+        chunks = chunks[4:]
         for r in range(4):
             w_cast(j1, r, "scalar")
-        for j in HEAD_TILES:
-            for pr in range(2):
-                for g in range(PASSES):
-                    w_turn(j, g, pr)
+        for g in range(PASSES):
+            w_turn(j0, g, 1)
+        for pr in range(2):
+            for g in range(PASSES):
+                w_turn(j1, g, pr)
         w_quant(j0)
         x_half(0)
         w_quant(j1)

@@ -146,8 +146,11 @@ def tile_gemmaattention_pa_kernel(
             wq[j] = const.tile([P, PASSES, N_TILE], U32, name="wq%d" % j, align_bytes=64)
             ws[j] = const.tile([P, PASSES, N_TILE], U8, name="ws%d" % j, align_bytes=64)
 
-        def turn(tiles, g):
-            tp = tpp.tile([P, 2, 2 * P], F32, name="tp", tag="tp")
+        def turn(tiles, g, spare=False):
+            if spare:
+                tp = accp.tile([P, 2, 2 * P], F32, name="acc", tag="acc")
+            else:
+                tp = tpp.tile([P, 2, 2 * P], F32, name="tp", tag="tp")
             for a in range(2):
                 words = tiles[a][:].bitcast(F32)
                 for u in range(2):
@@ -156,20 +159,23 @@ def tile_gemmaattention_pa_kernel(
                     )
             return tp
 
-        def x_half(half):
-            xg = grp.tile([P, 8 * N_TILE], BF16, name="grouped", tag="grouped", align_bytes=64)
-            for pr in range(2):
-                for g in range(PASSES):
-                    tp = turn((xr[half * 4 + pr * 2], xr[half * 4 + pr * 2 + 1]), g)
-                    c0 = (pr * PASSES + g) * 512
-                    nc.scalar.copy(
-                        out=xg[:].bitcast(F32)[:, c0 : c0 + 512].rearrange("p (r u) -> p r u", u=2),
-                        in_=tp[:].rearrange("p u r -> p r u"),
-                    )
+        xgs = {}
+
+        def x_turn(half, pr, g):
+            if (pr, g) == (0, 0):
+                xgs[half] = grp.tile([P, 8 * N_TILE], BF16, name="grouped", tag="grouped", align_bytes=64)
+            tp = turn((xr[half * 4 + pr * 2], xr[half * 4 + pr * 2 + 1]), g, True)
+            c0 = (pr * PASSES + g) * 512
+            nc.scalar.copy(
+                out=xgs[half][:].bitcast(F32)[:, c0 : c0 + 512].rearrange("p (r u) -> p r u", u=2),
+                in_=tp[:].rearrange("p u r -> p r u"),
+            )
+
+        def x_quant(half):
             nc.vector.quantize_mx(
                 out=xq[half][:].rearrange("p a g c -> p (a g c)").bitcast(FP8X4),
                 scales=xs[half][:].rearrange("p a g c -> p (a g c)"),
-                in_=xg[:],
+                in_=xgs[half][:],
             )
 
         wbf = {}
@@ -178,10 +184,15 @@ def tile_gemmaattention_pa_kernel(
         def w_cast(j, r, engine):
             wbf[(j, r)] = wbfp.tile([P, K], BF16, name="wbf", tag="wbf")
             src = wb[j][:, r, :].bitcast(FP8)
-            if engine == "vector":
-                nc.vector.tensor_copy(out=wbf[(j, r)][:], in_=src)
-            else:
-                nc.scalar.copy(out=wbf[(j, r)][:], in_=src)
+            nc.scalar.copy(out=wbf[(j, r)][:], in_=src)
+
+        def w_cast_first(j):
+            for r in range(2):
+                wbf[(j, r)] = wbfp.tile([P, K], BF16, name="wbf", tag="wbf")
+            for g in range(PASSES):
+                for r in range(2):
+                    ks = slice(g * 512, (g + 1) * 512)
+                    nc.vector.tensor_copy(out=wbf[(j, r)][:, ks], in_=wb[j][:, r, ks].bitcast(FP8))
 
         def w_turn(j, g, pr):
             if (g, pr) == (0, 0):
@@ -268,8 +279,7 @@ def tile_gemmaattention_pa_kernel(
         late = []
 
         j0, j1 = HEAD_TILES
-        w_cast(j0, 0, "vector")
-        w_cast(j0, 1, "vector")
+        w_cast_first(j0)
         w_cast(j0, 2, "scalar")
         w_cast(j0, 3, "scalar")
         for g in range(PASSES):
@@ -286,10 +296,14 @@ def tile_gemmaattention_pa_kernel(
         for pr in range(2):
             for g in range(PASSES):
                 w_turn(j1, g, pr)
+                x_turn(0, pr, g)
+        for pr in range(2):
+            for g in range(PASSES):
+                x_turn(1, pr, g)
         w_quant(j0)
-        x_half(0)
+        x_quant(0)
         w_quant(j1)
-        x_half(1)
+        x_quant(1)
         make_gains("k")
 
         values = [(i, j) for j in (6, 7) for i in range(TOK_TILES)]

from contextlib import ExitStack

import concourse.mybir as mybir
from concourse.masks import make_identity

F32 = mybir.dt.float32
BF16 = mybir.dt.bfloat16
U32 = mybir.dt.uint32
U8 = mybir.dt.uint8
FP8 = mybir.dt.float8_e4m3fn
FP8X4 = mybir.dt.float8_e4m3fn_x4
ALU = mybir.AluOpType
ACT = mybir.ActivationFunctionType

P = 128
S = 1024
K = 1024
N = 4096
HD = 256
HALF = 128
EPS = 1e-6
PASSES = 2
TOK_TILES = 8
N_TILE = 512
FLOPS = 2 * S * K * N

HEAD_TILES = (0, 6)
LOOP_TILES = (1, 2, 3, 7, 4, 5)
PERIOD = 8
LATE_ADDS = 3


def tile_gemmaattention_pa_kernel(
    tc, x, qkv_w_bytes, qkv_w_scale, q_norm_w, k_norm_w, freqs_cos, freqs_sin, out_0, out_1, out_2
):
    nc = tc.nc
    x2 = x.rearrange("o s k -> (o s) k")
    outs = (
        out_0.rearrange("o s h d -> (o s) (h d)"),
        out_1.rearrange("o s h d -> (o s) (h d)"),
        out_2.rearrange("o s h d -> (o s) (h d)"),
    )

    with ExitStack() as ctx:
        const = ctx.enter_context(tc.tile_pool(name="const", bufs=1))
        wbfp = ctx.enter_context(tc.tile_pool(name="wbfp", bufs=8))
        grp = ctx.enter_context(tc.tile_pool(name="grp", bufs=4))
        epi = ctx.enter_context(tc.tile_pool(name="epi", bufs=4))
        stat = ctx.enter_context(tc.tile_pool(name="stat", bufs=6))
        tpp = ctx.enter_context(tc.psum_pool(name="tpp", bufs=3))
        accp = ctx.enter_context(tc.psum_pool(name="accp", bufs=5))
        ctx.enter_context(tc.manual_schedule())

        s4 = const.tile([P, PASSES, 4], F32, name="s4")
        nc.scalar.dma_start(out=s4[:], in_=qkv_w_scale.rearrange("o (g p t) -> p (o g) t", p=P, t=4))
        cosb = const.tile([P, TOK_TILES, HALF], BF16, name="cosb")
        sinb = const.tile([P, TOK_TILES, HALF], BF16, name="sinb")
        wrow = const.tile([P, 2 * HD], BF16, name="wrow")
        nc.gpsimd.memset(wrow[:], 0.0)
        nc.scalar.dma_start(out=wrow[0:1, 0:HD], in_=q_norm_w.rearrange("(o d) -> o d", o=1))
        nc.scalar.dma_start(out=wrow[0:1, HD : 2 * HD], in_=k_norm_w.rearrange("(o d) -> o d", o=1))
        ones = const.tile([P, P], BF16, name="ones")
        nc.gpsimd.memset(ones[:], 1.0)

        def load_trig(i0):
            for trig, src in ((cosb, freqs_cos), (sinb, freqs_sin)):
                nc.sync.dma_start(
                    out=trig[:, i0 : i0 + 4, :], in_=src.rearrange("(i p) d -> p i d", p=P)[:, i0 : i0 + 4, :]
                )

        wb = {}
        xr = {}

        def load_w(j, pieces):
            wb[j] = const.tile([P, 4, K], U8, name="wb%d" % j)
            rt = 4 // pieces
            for c in range(pieces):
                nc.sync.dma_start(
                    out=wb[j][:, c * rt : (c + 1) * rt, :],
                    in_=qkv_w_bytes[j * N_TILE + c * rt * P : j * N_TILE + (c + 1) * rt * P, :].rearrange(
                        "(r p) k -> p r k", p=P
                    ),
                )

        load_w(HEAD_TILES[0], 2)
        load_trig(0)
        load_w(HEAD_TILES[1], 1)
        for i in range(TOK_TILES):
            xr[i] = const.tile([P, K], BF16, name="xr%d" % i)
            nc.sync.dma_start(out=xr[i][:], in_=x2[i * P : (i + 1) * P, :])
        load_trig(4)
        for j in LOOP_TILES:
            load_w(j, 1)

        one = const.tile([P, 1], F32, name="one")
        nc.vector.memset(one[:], 1.0)
        warm = const.tile([P, 1], F32, name="warm")
        nc.scalar.activation(out=warm[:], in_=one[:], func=ACT.Abs_reciprocal_sqrt)
        ident = const.tile([P, P], F32, name="ident")
        make_identity(nc, ident[:])

        tabs = {}
        gains = {}
        for tag in ("q", "k"):
            tabs[tag] = const.tile([P, TOK_TILES, 2 * HD], F32, name="tab" + tag)

        gall = const.tile([P, 2, HD], F32, name="gall")

        def spread_gains():
            wall = accp.tile([P, 2 * HD], F32, name="acc", tag="acc")
            nc.tensor.matmul(out=wall[:], lhsT=ones[:], rhs=wrow[:], start=True, stop=True)
            nc.scalar.activation(
                out=gall[:].rearrange("p t d -> p (t d)"), in_=wall[:], func=ACT.Copy, bias=1.0, scale=1.0
            )

        def make_gains(tag):
            gp = gall[:, 0 if tag == "q" else 1, :]
            gm = const.tile([P, HD], F32, name="gm" + tag)
            nc.gpsimd.tensor_scalar(
                out=gm[:, 0:HALF], in0=gp[:, 0:HALF], scalar1=1.0, scalar2=0.0, op0=ALU.mult, op1=ALU.add
            )
            nc.gpsimd.tensor_scalar(
                out=gm[:, HALF:HD], in0=gp[:, HALF:HD], scalar1=-1.0, scalar2=0.0, op0=ALU.mult, op1=ALU.add
            )
            gains[tag] = (gp, gm[:])

        def table_chunk(tag, i0, part):
            trig = (cosb, sinb)[part]
            nc.gpsimd.tensor_tensor(
                out=tabs[tag][:, i0 : i0 + 2, part * HD : (part + 1) * HD].rearrange("p i (a d) -> p i a d", a=2),
                in0=trig[:, i0 : i0 + 2, :].unsqueeze(2).to_broadcast([P, 2, 2, HALF]),
                in1=gains[tag][part].rearrange("p (a d) -> p a d", a=2).unsqueeze(1).to_broadcast([P, 2, 2, HALF]),
                op=ALU.mult,
            )

        chunks = [(tag, i0, part) for tag in ("q", "k") for i0 in range(0, TOK_TILES, 2) for part in range(2)]

        xq = {}
        xs = {}
        for half in range(2):
            xq[half] = const.tile([P, 2, PASSES, 2 * P], U32, name="xq%d" % half, align_bytes=64)
            xs[half] = const.tile([P, 2, PASSES, 2 * P], U8, name="xs%d" % half, align_bytes=64)
        wq = {}
        ws = {}
        for j in range(8):
            wq[j] = const.tile([P, PASSES, N_TILE], U32, name="wq%d" % j, align_bytes=64)
            ws[j] = const.tile([P, PASSES, N_TILE], U8, name="ws%d" % j, align_bytes=64)

        def turn(tiles, g, spare=False):
            if spare:
                tp = accp.tile([P, 2, 2 * P], F32, name="acc", tag="acc")
            else:
                tp = tpp.tile([P, 2, 2 * P], F32, name="tp", tag="tp")
            for a in range(2):
                words = tiles[a][:].bitcast(F32)
                for u in range(2):
                    nc.tensor.transpose(
                        tp[:, u, a * P : (a + 1) * P], words[:, 256 * g + u : 256 * (g + 1) : 2], ident[:]
                    )
            return tp

        xgs = {}

        def x_turn(half, pr, g):
            if (pr, g) == (0, 0):
                xgs[half] = grp.tile([P, 8 * N_TILE], BF16, name="grouped", tag="grouped", align_bytes=64)
            tp = turn((xr[half * 4 + pr * 2], xr[half * 4 + pr * 2 + 1]), g, True)
            c0 = (pr * PASSES + g) * 512
            nc.scalar.copy(
                out=xgs[half][:].bitcast(F32)[:, c0 : c0 + 512].rearrange("p (r u) -> p r u", u=2),
                in_=tp[:].rearrange("p u r -> p r u"),
            )

        def x_quant(half):
            nc.vector.quantize_mx(
                out=xq[half][:].rearrange("p a g c -> p (a g c)").bitcast(FP8X4),
                scales=xs[half][:].rearrange("p a g c -> p (a g c)"),
                in_=xgs[half][:],
            )

        wbf = {}
        wgr = {}

        def w_cast(j, r, engine):
            wbf[(j, r)] = wbfp.tile([P, K], BF16, name="wbf", tag="wbf")
            src = wb[j][:, r, :].bitcast(FP8)
            nc.scalar.copy(out=wbf[(j, r)][:], in_=src)

        def w_cast_first(j):
            for r in range(2):
                wbf[(j, r)] = wbfp.tile([P, K], BF16, name="wbf", tag="wbf")
            for g in range(PASSES):
                for r in range(2):
                    ks = slice(g * 512, (g + 1) * 512)
                    nc.vector.tensor_copy(out=wbf[(j, r)][:, ks], in_=wb[j][:, r, ks].bitcast(FP8))

        def w_turn(j, g, pr):
            if (g, pr) == (0, 0):
                wgr[j] = grp.tile([P, 8 * N_TILE], BF16, name="grouped", tag="grouped", align_bytes=64)
            tp = turn((wbf[(j, pr * 2)], wbf[(j, pr * 2 + 1)]), g)
            c0 = g * 2048 + pr * 1024
            nc.vector.tensor_tensor(
                out=wgr[j][:, c0 : c0 + 1024].rearrange("p (n u e) -> p n u e", u=2, e=2),
                in0=tp[:].bitcast(BF16).rearrange("p u (n e) -> p n u e", e=2),
                in1=s4[:, g, :].rearrange("p (o u e) -> p o u e", o=1, u=2).to_broadcast([P, 2 * P, 2, 2]),
                op=ALU.mult,
            )

        def w_quant(j):
            nc.vector.quantize_mx(
                out=wq[j][:].rearrange("p g c -> p (g c)").bitcast(FP8X4),
                scales=ws[j][:].rearrange("p g c -> p (g c)"),
                in_=wgr[j][:],
            )

        def step(i, j, quant_tile, late_add):
            acc = accp.tile([P, N_TILE], F32, name="acc", tag="acc")
            rows = slice(i * P, (i + 1) * P)
            cols = slice((i % 2) * P, (i % 2 + 1) * P)
            for g in range(PASSES):
                nc.tensor.matmul_mx(
                    out=acc[:],
                    lhsT=xq[i // 4][:, (i % 4) // 2, g, cols].bitcast(FP8X4),
                    lhsT_scale=xs[i // 4][:, (i % 4) // 2, g, cols],
                    rhs=wq[j][:, g, :].bitcast(FP8X4),
                    rhs_scale=ws[j][:, g, :],
                    start=(g == 0),
                    stop=(g == PASSES - 1),
                )
            if j >= 6:
                res = epi.tile([P, N_TILE], F32, name="resv", tag="resv", bufs=3)
                nc.scalar.copy(out=res[:], in_=acc[:])
                dst = outs[2][rows, (j - 6) * N_TILE : (j - 5) * N_TILE]
            else:
                tab = tabs["q" if j < 4 else "k"]
                ms = stat.tile([P, 2], F32, name="ms", tag="ms")
                for h in range(2):
                    junk = stat.tile([P, HD], BF16, name="junk", tag="junk")
                    nc.scalar.activation(
                        out=junk[:],
                        in_=acc[:, h * HD : (h + 1) * HD],
                        func=ACT.Square,
                        scale=0.0625,
                        accum_out=ms[:, h : h + 1],
                    )
                rs = stat.tile([P, 2], F32, name="rs", tag="rs")
                nc.scalar.activation(out=rs[:], in_=ms[:], func=ACT.Abs_reciprocal_sqrt, bias=EPS, scale=1.0)
                pq = epi.tile([P, 2, 2, 2, HALF], F32, name="pq", tag="pq")
                for h in range(2):
                    nc.vector.scalar_tensor_tensor(
                        out=pq[:, h].rearrange("p r a d -> p r (a d)"),
                        in0=acc[:, h * HD : (h + 1) * HD].unsqueeze(1).to_broadcast([P, 2, HD]),
                        scalar=rs[:, h : h + 1],
                        in1=tab[:, i, :].rearrange("p (r c) -> p r c", r=2),
                        op0=ALU.mult,
                        op1=ALU.mult,
                    )
                    if h == 0 and quant_tile is not None:
                        w_quant(quant_tile)
                if j < 4:
                    dst = outs[0][rows, j * N_TILE : (j + 1) * N_TILE]
                else:
                    dst = outs[1][rows, (j - 4) * N_TILE : (j - 3) * N_TILE]
                if late_add:
                    late.append((pq, dst))
                    return
                res = epi.tile([P, N_TILE], F32, name="res", tag="res")
                add_halves(nc.gpsimd, res, pq)
            nc.sync.dma_start(out=dst, in_=res[:])

        def add_halves(engine, res, pq):
            engine.tensor_tensor(
                out=res[:].rearrange("p (h a d) -> p h a d", h=2, a=2),
                in0=pq[:, :, 0, :, :],
                in1=pq[:, :, 1, ::-1, :],
                op=ALU.add,
            )

        late = []

        j0, j1 = HEAD_TILES
        w_cast_first(j0)
        w_cast(j0, 2, "scalar")
        w_cast(j0, 3, "scalar")
        for g in range(PASSES):
            w_turn(j0, g, 0)
        spread_gains()
        make_gains("q")
        for n in range(4):
            table_chunk(*chunks[n])
        chunks = chunks[4:]
        for r in range(4):
            w_cast(j1, r, "scalar")
        for g in range(PASSES):
            w_turn(j0, g, 1)
        for pr in range(2):
            for g in range(PASSES):
                w_turn(j1, g, pr)
                x_turn(0, pr, g)
        for pr in range(2):
            for g in range(PASSES):
                x_turn(1, pr, g)
        w_quant(j0)
        x_quant(0)
        w_quant(j1)
        x_quant(1)
        make_gains("k")

        values = [(i, j) for j in (6, 7) for i in range(TOK_TILES)]
        slots = []
        for n in range(48):
            slots.append((n % TOK_TILES, n // TOK_TILES))
            if n % 3 == 2:
                slots.append(values[n // 3])
        rope_steps = 0
        waiting = None
        for n, slot in enumerate(slots):
            i, j = slot
            if j < 6:
                step(i, j, waiting, rope_steps >= 48 - LATE_ADDS)
                rope_steps += 1
                if chunks and (rope_steps <= 2 or waiting is not None):
                    table_chunk(*chunks[0])
                    table_chunk(*chunks[1])
                    chunks = chunks[2:]
                waiting = None
            else:
                step(i, j, None, False)
            if n // PERIOD < len(LOOP_TILES):
                jn = LOOP_TILES[n // PERIOD]
                phase = n % PERIOD
                if phase == 0:
                    w_cast(jn, 0, "scalar")
                    w_cast(jn, 1, "scalar")
                elif phase == 1:
                    w_turn(jn, 0, 0)
                    w_turn(jn, 1, 0)
                    w_cast(jn, 2, "scalar")
                    w_cast(jn, 3, "scalar")
                elif phase == 6:
                    w_turn(jn, 0, 1)
                    w_turn(jn, 1, 1)
                    waiting = jn
        assert not chunks
        for pq, dst in late:
            res = epi.tile([P, N_TILE], F32, name="resw", tag="resw", bufs=LATE_ADDS)
            add_halves(nc.vector, res, pq)
            nc.sync.dma_start(out=dst, in_=res[:])
